import numpy as np
import ml_dtypes


def mxq(x, axis, fmt="e4m3"):
    dtype, down = {"e4m3": (ml_dtypes.float8_e4m3fn, 7), "e5m2": (ml_dtypes.float8_e5m2, 14)}[fmt]
    v = np.moveaxis(np.asarray(x, np.float32).astype(ml_dtypes.bfloat16).astype(np.float64), axis, -1)
    blocks = v.reshape(v.shape[:-1] + (-1, 32))
    amax = np.abs(blocks).max(-1, keepdims=True)
    byte = np.maximum(np.where(amax > 0, np.frexp(amax)[1] - 1 + 127, 0) - down, 1)
    scale = np.exp2(byte - 127.0)
    codes = (blocks / scale).astype(np.float32).astype(dtype).astype(np.float64)
    return np.moveaxis((codes * scale).reshape(v.shape), -1, axis)


WIDE = False


def mx_kscale(k):
    if not WIDE:
        return np.ones(k)
    levels = np.array([10, -10, 5, -5, 0])
    a = np.random.permutation(np.resize(levels, k // 512 * 4)).reshape(k // 512, 4)
    idx = np.arange(k)
    return np.exp2(a[idx // 512, idx % 128 // 32])


BF16 = ml_dtypes.bfloat16


def bf(x):
    return np.asarray(x, np.float32).astype(BF16)


def f64(x):
    return np.asarray(x).astype(np.float64)


B, F, C, N = 2048, 4, 512, 128
DIAG = 3.0 * np.log(C)
LAM = 3.0
TANH_RMS = 0.628
NH = N // 2
X0 = 5.0


def setup_inputs():
    t = mx_kscale(C)
    wide = float(t.max() > 1.0)
    x = np.random.standard_normal((B, F, N)) * LAM / np.sqrt(DIAG)
    p = np.tanh(np.random.standard_normal((F, C, N))) * np.sqrt(DIAG / N) / TANH_RMS
    x[:, :, 0] += wide * (X0 - x[:, :, 0])
    x[:, :, NH:] /= t.max() ** 2
    p[:, :, 0] -= np.log(t) / X0
    p[:, :, NH:] *= t[:, None]
    return {"x": bf(x), "patterns": bf(p)}


def reference(x, patterns):
    xt = f64(x).transpose(1, 0, 2)
    p = f64(patterns)
    gram = p @ p.transpose(0, 2, 1)
    s = xt @ p.transpose(0, 2, 1)
    e = np.exp(s - s.max(-1, keepdims=True))
    y = (mxq(e, 2, "e4m3") @ mxq(gram.transpose(0, 2, 1), 1, "e4m3")) / e.sum(-1, keepdims=True)
    return y.transpose(1, 0, 2)

@@ -1,0 +1,231 @@
+from contextlib import ExitStack
+
+import concourse.mybir as mybir
+from concourse.masks import make_identity
+
+F32 = mybir.dt.float32
+BF16 = mybir.dt.bfloat16
+U32 = mybir.dt.uint32
+U8 = mybir.dt.uint8
+FP8X4 = mybir.dt.float8_e4m3fn_x4
+ACT = mybir.ActivationFunctionType
+ALU = mybir.AluOpType
+AX = mybir.AxisListType
+
+P = 128
+B, F, C, N = 2048, 4, 512, 128
+T = C // P
+NB = B // P
+NT = NB * F
+NQ = NT // 2
+NG = F * T
+LAG = 4
+FLOPS = 2 * (B * F * C * N + F * C * C * N + B * F * C * C)
+
+
+def tile_hopfieldlayer_pa_t_kernel(tc, x, patterns, out):
+    nc = tc.nc
+    with ExitStack() as ctx:
+        ctx.enter_context(tc.manual_schedule())
+        keep = ctx.enter_context(tc.tile_pool(name="keep", bufs=1))
+        work = ctx.enter_context(tc.tile_pool(name="work", bufs=3))
+        small = ctx.enter_context(tc.tile_pool(name="small", bufs=6))
+        outs = ctx.enter_context(tc.tile_pool(name="outs", bufs=4))
+        ps_s = ctx.enter_context(tc.psum_pool(name="ps_s", bufs=4))
+        ps_t = ctx.enter_context(tc.psum_pool(name="ps_t", bufs=2))
+        ps_y = ctx.enter_context(tc.psum_pool(name="ps_y", bufs=2))
+
+        x_v = x.rearrange("(p i) f n -> p i (f n)", i=NB)
+        p_v = patterns.rearrange("f (t p) n -> p f t n", p=P)
+        out_v = out.rearrange("(p i) f c -> p i f c", i=NB)
+
+        p_sb = keep.tile([P, F, T, N], BF16)
+        x_sb = keep.tile([P, NB, F * N], BF16)
+        nc.sync.dma_start(out=p_sb[:, 0:2], in_=p_v[:, 0:2])
+        nc.sync.dma_start(out=x_sb[:, 0:2, :], in_=x_v[:, 0:2, :])
+        nc.sync.dma_start(out=p_sb[:, 2:4], in_=p_v[:, 2:4])
+        nc.sync.dma_start(out=x_sb[:, 2:4, :], in_=x_v[:, 2:4, :])
+        for i0 in (4, 8, 12):
+            nc.sync.dma_start(out=x_sb[:, i0 : i0 + 4, :], in_=x_v[:, i0 : i0 + 4, :])
+
+        ident = keep.tile([P, P], BF16)
+        make_identity(nc, ident[:])
+        warm_in = keep.tile([P, 1], F32)
+        warm_out = keep.tile([P, 1], F32)
+        nc.vector.memset(warm_in[:], 0.0)
+        nc.scalar.activation(out=warm_out[:], in_=warm_in[:], func=ACT.Exp)
+
+        pt = keep.tile([P, F, C], BF16)
+        xt = keep.tile([P, NB, F, P], BF16)
+        g_codes = keep.tile([P, F, C], U32, align_bytes=64)
+        g_scales = keep.tile([P, F, C], U8, align_bytes=64)
+
+        def transposes(src):
+            tp = ps_t.tile([P, 8, P], BF16, tag="tp", name="tp")
+            for r in range(8):
+                nc.tensor.transpose(out=tp[:, r, :], in_=src(r), identity=ident[:])
+            return tp
+
+        xtp = {}
+
+        def x_transposes(ii):
+            xtp[ii] = transposes(lambda r: x_sb[:, 2 * ii + r // F, (r % F) * N : (r % F + 1) * N])
+
+        def x_copy(ii):
+            nc.scalar.copy(out=xt[:, 2 * ii : 2 * ii + 2].rearrange("n i f b -> n (i f) b"), in_=xtp[ii][:])
+
+        s_ps, mn, ssum, e_sb, et_ps, grp, codes, scales, rs, y_ps, o_sb, gg = {}, {}, {}, {}, {}, {}, {}, {}, {}, {}, {}, {}
+
+        def st_a(k):
+            i, f = k // F, k % F
+            s_ps[k] = ps_s.tile([P, C], F32, tag="s", name="s")
+            nc.tensor.matmul(out=s_ps[k][:], lhsT=xt[:, i, f, :], rhs=pt[:, f, :], start=True, stop=True)
+
+        def st_b(k):
+            q, j = k // 2, k % 2
+            if j == 0:
+                mn[q] = small.tile([P, 2], F32, tag="mn", name="mn")
+            nc.vector.tensor_reduce(out=mn[q][:, j : j + 1], in_=s_ps[k][:], axis=AX.X, op=ALU.max, negate=True)
+
+        def st_c(k):
+            q, j = k // 2, k % 2
+            if j == 0:
+                e_sb[q] = work.tile([P, 2 * T, P], BF16, tag="e", name="e")
+                ssum[q] = small.tile([P, 2], F32, tag="ssum", name="ssum")
+            nc.scalar.activation(
+                out=e_sb[q][:, j * T : (j + 1) * T, :].rearrange("b t p -> b (t p)"),
+                in_=s_ps[k][:],
+                func=ACT.Exp,
+                bias=mn[q][:, j : j + 1],
+                scale=1.0,
+                accum_out=ssum[q][:, j : j + 1],
+            )
+
+        def st_d(q):
+            et_ps[q] = transposes(lambda r: e_sb[q][:, r, :])
+
+        def st_e(q):
+            grp[q] = work.tile([P, 2, P, T], BF16, tag="grp", name="grp", align_bytes=64)
+            nc.vector.tensor_copy(out=grp[q][:], in_=et_ps[q][:].rearrange("p (j t) b -> p j b t", t=T))
+
+        def st_f(q):
+            codes[q] = work.tile([P, 2 * P], U32, tag="codes", name="codes", align_bytes=64)
+            scales[q] = work.tile([P, 2 * P], U8, tag="scales", name="scales", align_bytes=64)
+            nc.vector.quantize_mx(
+                out=codes[q][:].bitcast(FP8X4),
+                scales=scales[q][:],
+                in_=grp[q][:].rearrange("p j b t -> p (j b t)"),
+            )
+            rs[q] = small.tile([P, 2], F32, tag="rs", name="rs")
+            nc.vector.reciprocal(out=rs[q][:], in_=ssum[q][:])
+
+        def st_g(k):
+            if k >= NT or k < -NG:
+                return
+            if k < 0:
+                f, cb = (k + NG) // T, (k + NG) % T
+                y_ps[k] = ps_y.tile([P, T, P], F32, tag="y", name="y")
+                for t in range(T):
+                    nc.tensor.matmul(
+                        out=y_ps[k][:, t, :],
+                        lhsT=pt[:, f, t * P : (t + 1) * P],
+                        rhs=pt[:, f, cb * P : (cb + 1) * P],
+                        start=True,
+                        stop=True,
+                    )
+                return
+            q, j, f = k // 2, k % 2, k % F
+            y_ps[k] = ps_y.tile([P, C], F32, tag="y", name="y")
+            nc.tensor.matmul_mx(
+                out=y_ps[k][:],
+                lhsT=codes[q][:, j * P : (j + 1) * P].bitcast(FP8X4),
+                lhsT_scale=scales[q][:, j * P : (j + 1) * P],
+                rhs=g_codes[:, f, :].bitcast(FP8X4),
+                rhs_scale=g_scales[:, f, :],
+                start=True,
+                stop=True,
+            )
+
+        def st_h(k, on_vector):
+            if k < -NG:
+                return
+            if k < 0:
+                f, cb = (k + NG) // T, (k + NG) % T
+                if cb == 0:
+                    gg[f] = work.tile([P, C, T], BF16, tag="gg", name="gg", align_bytes=64, bufs=2)
+                dst = gg[f][:, cb * P : (cb + 1) * P, :]
+                src = y_ps[k][:].rearrange("p t c -> p c t")
+                if on_vector:
+                    nc.vector.tensor_copy(out=dst, in_=src)
+                else:
+                    nc.scalar.copy(out=dst, in_=src)
+                return
+            q, j = k // 2, k % 2
+            if j == 0:
+                o_sb[q] = outs.tile([P, 2, C], F32, tag="o", name="o")
+            if on_vector:
+                nc.vector.tensor_scalar_mul(out=o_sb[q][:, j, :], in0=y_ps[k][:], scalar1=rs[q][:, j : j + 1])
+            else:
+                nc.scalar.activation(out=o_sb[q][:, j, :], in_=y_ps[k][:], func=ACT.Copy, scale=rs[q][:, j : j + 1])
+
+        def gram_quant(f):
+            nc.vector.quantize_mx(
+                out=g_codes[:, f, :].bitcast(FP8X4),
+                scales=g_scales[:, f, :],
+                in_=gg[f][:].rearrange("p c t -> p (c t)"),
+            )
+
+        def store(q, j0, j1):
+            i, f0 = q // 2, 2 * (q % 2)
+            nc.sync.dma_start(out=out_v[:, i, f0 + j0 : f0 + j1, :], in_=o_sb[q][:, j0:j1, :])
+
+        ptp = transposes(lambda r: p_sb[:, r // T, r % T, :])
+        nc.vector.tensor_copy(out=pt[:, 0:2, :].rearrange("n f (t p) -> n (f t) p", p=P), in_=ptp[:])
+        x_transposes(0)
+        x_copy(0)
+        ptp = transposes(lambda r: p_sb[:, 2 + r // T, r % T, :])
+        nc.vector.tensor_copy(out=pt[:, 2:4, :].rearrange("n f (t p) -> n (f t) p", p=P), in_=ptp[:])
+        st_g(-NG)
+        st_g(-NG + 1)
+
+        def live(q):
+            return 0 <= q < NQ
+
+        for u in range(-NG // 4, NQ + LAG):
+            w = u - LAG
+            vector_helps = u < 2 or u >= NQ + 2
+            if live(u):
+                st_b(2 * u)
+            if live(u - 2):
+                st_e(u - 2)
+            if u % 2 == 0 and 0 <= (u + 2) // 2 < F:
+                gram_quant((u + 2) // 2)
+            if live(u):
+                st_b(2 * u + 1)
+            if live(u - 2):
+                st_f(u - 2)
+            if live(u - 1):
+                st_c(2 * u - 2)
+            if -1 <= u < NQ - 1:
+                st_a(2 * u + 2)
+            if u == NQ:
+                st_c(2 * u - 1)
+                st_d(u - 1)
+            st_h(2 * w, False)
+            st_g(2 * w + 2)
+            if live(u - 1) and u < NQ:
+                st_c(2 * u - 1)
+                st_d(u - 1)
+            if -1 <= u < NQ - 1:
+                st_a(2 * u + 3)
+            st_h(2 * w + 1, vector_helps)
+            if w == NQ - 1:
+                store(w, 0, 1)
+                store(w, 1, 2)
+            elif w >= 0:
+                store(w, 0, 2)
+            st_g(2 * w + 3)
+            if u % 4 == 2 and 0 < (u + 2) // 4 < NB // 2:
+                x_copy((u + 2) // 4)
+            if u % 4 == 1 and 0 < (u + 3) // 4 < NB // 2:
+                x_transposes((u + 3) // 4)

@@ -19,7 +19,7 @@ NB = B // P
 NT = NB * F
 NQ = NT // 2
 NG = F * T
-LAG = 4
+LAG = 6
 FLOPS = 2 * (B * F * C * N + F * C * C * N + B * F * C * C)
 
 
@@ -71,10 +71,14 @@ def tile_hopfieldlayer_pa_t_kernel(tc, x, patterns, out):
         def x_transposes(ii):
             xtp[ii] = transposes(lambda r: x_sb[:, 2 * ii + r // F, (r % F) * N : (r % F + 1) * N])
 
-        def x_copy(ii):
-            nc.scalar.copy(out=xt[:, 2 * ii : 2 * ii + 2].rearrange("n i f b -> n (i f) b"), in_=xtp[ii][:])
+        def x_copy(ii, on_vector):
+            dst = xt[:, 2 * ii : 2 * ii + 2].rearrange("n i f b -> n (i f) b")
+            if on_vector:
+                nc.vector.tensor_copy(out=dst, in_=xtp[ii][:])
+            else:
+                nc.scalar.copy(out=dst, in_=xtp[ii][:])
 
-        s_ps, mn, ssum, e_sb, et_ps, grp, codes, scales, rs, y_ps, o_sb, gg = {}, {}, {}, {}, {}, {}, {}, {}, {}, {}, {}, {}
+        s_ps, mn, ssum, e_sb, et_ps, grp, codes, scales, rs, y_ps, o_sb, gg, stg = {}, {}, {}, {}, {}, {}, {}, {}, {}, {}, {}, {}, {}
 
         def st_a(k):
             i, f = k // F, k % F
@@ -91,33 +95,47 @@ def tile_hopfieldlayer_pa_t_kernel(tc, x, patterns, out):
             q, j = k // 2, k % 2
             if j == 0:
                 e_sb[q] = work.tile([P, 2 * T, P], BF16, tag="e", name="e")
-                ssum[q] = small.tile([P, 2], F32, tag="ssum", name="ssum")
+            if k % F == 0:
+                ssum[k // F] = small.tile([P, F], F32, tag="ssum", name="ssum")
             nc.scalar.activation(
                 out=e_sb[q][:, j * T : (j + 1) * T, :].rearrange("b t p -> b (t p)"),
                 in_=s_ps[k][:],
                 func=ACT.Exp,
                 bias=mn[q][:, j : j + 1],
                 scale=1.0,
-                accum_out=ssum[q][:, j : j + 1],
+                accum_out=ssum[k // F][:, k % F : k % F + 1],
             )
 
         def st_d(q):
             et_ps[q] = transposes(lambda r: e_sb[q][:, r, :])
 
-        def st_e(q):
-            grp[q] = work.tile([P, 2, P, T], BF16, tag="grp", name="grp", align_bytes=64)
-            nc.vector.tensor_copy(out=grp[q][:], in_=et_ps[q][:].rearrange("p (j t) b -> p j b t", t=T))
+        def st_e1(q):
+            stg[q] = work.tile([P, 2 * T, P], BF16, tag="stg", name="stg", bufs=2)
+            nc.vector.tensor_copy(out=stg[q][:], in_=et_ps[q][:])
 
-        def st_f(q):
-            codes[q] = work.tile([P, 2 * P], U32, tag="codes", name="codes", align_bytes=64)
-            scales[q] = work.tile([P, 2 * P], U8, tag="scales", name="scales", align_bytes=64)
-            nc.vector.quantize_mx(
-                out=codes[q][:].bitcast(FP8X4),
-                scales=scales[q][:],
-                in_=grp[q][:].rearrange("p j b t -> p (j b t)"),
+        def st_e2(q):
+            i, h = q // 2, q % 2
+            if h == 0:
+                grp[i] = work.tile([P, F, P, T], BF16, tag="grp", name="grp", align_bytes=64, bufs=1)
+            nc.gpsimd.tensor_scalar(
+                out=grp[i][:, 2 * h : 2 * h + 2],
+                in0=stg[q][:].rearrange("p (j t) b -> p j b t", t=T),
+                scalar1=1.0,
+                scalar2=0.0,
+                op0=ALU.mult,
+                op1=ALU.add,
             )
-            rs[q] = small.tile([P, 2], F32, tag="rs", name="rs")
-            nc.vector.reciprocal(out=rs[q][:], in_=ssum[q][:])
+
+        def st_f(i):
+            codes[i] = work.tile([P, F * P], U32, tag="codes", name="codes", align_bytes=64)
+            scales[i] = work.tile([P, F * P], U8, tag="scales", name="scales", align_bytes=64)
+            nc.vector.quantize_mx(
+                out=codes[i][:].bitcast(FP8X4),
+                scales=scales[i][:],
+                in_=grp[i][:].rearrange("p f b t -> p (f b t)"),
+            )
+            rs[i] = small.tile([P, F], F32, tag="rs", name="rs")
+            nc.vector.reciprocal(out=rs[i][:], in_=ssum[i][:])
 
         def st_g(k):
             if k >= NT or k < -NG:
@@ -138,8 +156,8 @@ def tile_hopfieldlayer_pa_t_kernel(tc, x, patterns, out):
             y_ps[k] = ps_y.tile([P, C], F32, tag="y", name="y")
             nc.tensor.matmul_mx(
                 out=y_ps[k][:],
-                lhsT=codes[q][:, j * P : (j + 1) * P].bitcast(FP8X4),
-                lhsT_scale=scales[q][:, j * P : (j + 1) * P],
+                lhsT=codes[k // F][:, f * P : (f + 1) * P].bitcast(FP8X4),
+                lhsT_scale=scales[k // F][:, f * P : (f + 1) * P],
                 rhs=g_codes[:, f, :].bitcast(FP8X4),
                 rhs_scale=g_scales[:, f, :],
                 start=True,
@@ -164,9 +182,11 @@ def tile_hopfieldlayer_pa_t_kernel(tc, x, patterns, out):
             if j == 0:
                 o_sb[q] = outs.tile([P, 2, C], F32, tag="o", name="o")
             if on_vector:
-                nc.vector.tensor_scalar_mul(out=o_sb[q][:, j, :], in0=y_ps[k][:], scalar1=rs[q][:, j : j + 1])
+                nc.vector.tensor_scalar_mul(out=o_sb[q][:, j, :], in0=y_ps[k][:], scalar1=rs[k // F][:, k % F : k % F + 1])
             else:
-                nc.scalar.activation(out=o_sb[q][:, j, :], in_=y_ps[k][:], func=ACT.Copy, scale=rs[q][:, j : j + 1])
+                nc.scalar.activation(
+                    out=o_sb[q][:, j, :], in_=y_ps[k][:], func=ACT.Copy, scale=rs[k // F][:, k % F : k % F + 1]
+                )
 
         def gram_quant(f):
             nc.vector.quantize_mx(
@@ -182,7 +202,7 @@ def tile_hopfieldlayer_pa_t_kernel(tc, x, patterns, out):
         ptp = transposes(lambda r: p_sb[:, r // T, r % T, :])
         nc.vector.tensor_copy(out=pt[:, 0:2, :].rearrange("n f (t p) -> n (f t) p", p=P), in_=ptp[:])
         x_transposes(0)
-        x_copy(0)
+        x_copy(0, False)
         ptp = transposes(lambda r: p_sb[:, 2 + r // T, r % T, :])
         nc.vector.tensor_copy(out=pt[:, 2:4, :].rearrange("n f (t p) -> n (f t) p", p=P), in_=ptp[:])
         st_g(-NG)
@@ -191,19 +211,23 @@ def tile_hopfieldlayer_pa_t_kernel(tc, x, patterns, out):
         def live(q):
             return 0 <= q < NQ
 
-        for u in range(-NG // 4, NQ + LAG):
+        for u in range(LAG - NG // 2, NQ + LAG):
             w = u - LAG
-            vector_helps = u < 2 or u >= NQ + 2
+            vector_helps = u < 1 or u >= NQ + 3
             if live(u):
                 st_b(2 * u)
             if live(u - 2):
-                st_e(u - 2)
-            if u % 2 == 0 and 0 <= (u + 2) // 2 < F:
-                gram_quant((u + 2) // 2)
+                st_e1(u - 2)
+            if u % 2 == 0 and live(u - 3):
+                st_f((u - 4) // 2)
+            if live(u - 2):
+                st_e2(u - 2)
+            if u % 2 == 0 and 0 <= u // 2 < F:
+                gram_quant(u // 2)
             if live(u):
                 st_b(2 * u + 1)
-            if live(u - 2):
-                st_f(u - 2)
+            if u % 4 == 1 and 0 < (u + 3) // 4 < NB // 2:
+                x_copy((u + 3) // 4, True)
             if live(u - 1):
                 st_c(2 * u - 2)
             if -1 <= u < NQ - 1:
@@ -225,7 +249,5 @@ def tile_hopfieldlayer_pa_t_kernel(tc, x, patterns, out):
             elif w >= 0:
                 store(w, 0, 2)
             st_g(2 * w + 3)
-            if u % 4 == 2 and 0 < (u + 2) // 4 < NB // 2:
-                x_copy((u + 2) // 4)
-            if u % 4 == 1 and 0 < (u + 3) // 4 < NB // 2:
-                x_transposes((u + 3) // 4)
+            if u % 4 == 0 and 0 < (u + 4) // 4 < NB // 2:
+                x_transposes((u + 4) // 4)

@@ -26,7 +26,6 @@ FLOPS = 2 * (B * F * C * N + F * C * C * N + B * F * C * C)
 def tile_hopfieldlayer_pa_t_kernel(tc, x, patterns, out):
     nc = tc.nc
     with ExitStack() as ctx:
-        ctx.enter_context(tc.manual_schedule())
         keep = ctx.enter_context(tc.tile_pool(name="keep", bufs=1))
         work = ctx.enter_context(tc.tile_pool(name="work", bufs=3))
         small = ctx.enter_context(tc.tile_pool(name="small", bufs=6))

@@ -20,12 +20,15 @@ NT = NB * F
 NQ = NT // 2
 NG = F * T
 LAG = 6
+HELP = 5
+WARM = 5
 FLOPS = 2 * (B * F * C * N + F * C * C * N + B * F * C * C)
 
 
 def tile_hopfieldlayer_pa_t_kernel(tc, x, patterns, out):
     nc = tc.nc
     with ExitStack() as ctx:
+        ctx.enter_context(tc.manual_schedule())
         keep = ctx.enter_context(tc.tile_pool(name="keep", bufs=1))
         work = ctx.enter_context(tc.tile_pool(name="work", bufs=3))
         small = ctx.enter_context(tc.tile_pool(name="small", bufs=6))
@@ -53,6 +56,12 @@ def tile_hopfieldlayer_pa_t_kernel(tc, x, patterns, out):
         warm_out = keep.tile([P, 1], F32)
         nc.vector.memset(warm_in[:], 0.0)
         nc.scalar.activation(out=warm_out[:], in_=warm_in[:], func=ACT.Exp)
+
+        zeros = keep.tile([P, C], BF16)
+        nc.vector.memset(zeros[:], 0.0)
+        idle = ps_s.tile([P, C], F32, tag="s", name="s")
+        for r in range(WARM):
+            nc.tensor.matmul(out=idle[:], lhsT=zeros[:, 0:P], rhs=zeros[:], start=True, stop=True)
 
         pt = keep.tile([P, F, C], BF16)
         xt = keep.tile([P, NB, F, P], BF16)
@@ -212,7 +221,7 @@ def tile_hopfieldlayer_pa_t_kernel(tc, x, patterns, out):
 
         for u in range(LAG - NG // 2, NQ + LAG):
             w = u - LAG
-            vector_helps = u < 1 or u >= NQ + 3
+            vector_helps = u < 1 or u >= NQ + 3 or (u >= LAG and u % HELP == 3)
             if live(u):
                 st_b(2 * u)
             if live(u - 2):

@@ -118,6 +118,8 @@ def tile_hopfieldlayer_pa_t_kernel(tc, x, patterns, out):
             et_ps[q] = transposes(lambda r: e_sb[q][:, r, :])
 
         def st_e1(q):
+            if q == NQ - 1:
+                return
             stg[q] = work.tile([P, 2 * T, P], BF16, tag="stg", name="stg", bufs=2)
             nc.vector.tensor_copy(out=stg[q][:], in_=et_ps[q][:])
 
@@ -125,6 +127,11 @@ def tile_hopfieldlayer_pa_t_kernel(tc, x, patterns, out):
             i, h = q // 2, q % 2
             if h == 0:
                 grp[i] = work.tile([P, F, P, T], BF16, tag="grp", name="grp", align_bytes=64, bufs=1)
+            if q == NQ - 1:
+                nc.vector.tensor_copy(
+                    out=grp[i][:, 2 * h : 2 * h + 2], in_=et_ps[q][:].rearrange("p (j t) b -> p j b t", t=T)
+                )
+                return
             nc.gpsimd.tensor_scalar(
                 out=grp[i][:, 2 * h : 2 * h + 2],
                 in0=stg[q][:].rearrange("p (j t) b -> p j b t", t=T),
@@ -146,22 +153,22 @@ def tile_hopfieldlayer_pa_t_kernel(tc, x, patterns, out):
             nc.vector.reciprocal(out=rs[i][:], in_=ssum[i][:])
 
         def st_g(k):
-            if k >= NT or k < -NG:
-                return
+            if k < 4 - NG or k >= NT - 2 * LAG + 2:
+                y_ps[k] = ps_s.tile([P, C], F32, tag="s", name="s")
+            else:
+                y_ps[k] = ps_y.tile([P, C], F32, tag="y", name="y")
             if k < 0:
                 f, cb = (k + NG) // T, (k + NG) % T
-                y_ps[k] = ps_y.tile([P, T, P], F32, tag="y", name="y")
                 for t in range(T):
                     nc.tensor.matmul(
-                        out=y_ps[k][:, t, :],
+                        out=y_ps[k][:, t * P : (t + 1) * P],
                         lhsT=pt[:, f, t * P : (t + 1) * P],
                         rhs=pt[:, f, cb * P : (cb + 1) * P],
                         start=True,
                         stop=True,
                     )
                 return
-            q, j, f = k // 2, k % 2, k % F
-            y_ps[k] = ps_y.tile([P, C], F32, tag="y", name="y")
+            f = k % F
             nc.tensor.matmul_mx(
                 out=y_ps[k][:],
                 lhsT=codes[k // F][:, f * P : (f + 1) * P].bitcast(FP8X4),
@@ -180,7 +187,7 @@ def tile_hopfieldlayer_pa_t_kernel(tc, x, patterns, out):
                 if cb == 0:
                     gg[f] = work.tile([P, C, T], BF16, tag="gg", name="gg", align_bytes=64, bufs=2)
                 dst = gg[f][:, cb * P : (cb + 1) * P, :]
-                src = y_ps[k][:].rearrange("p t c -> p c t")
+                src = y_ps[k][:].rearrange("p (t c) -> p c t", t=T)
                 if on_vector:
                     nc.vector.tensor_copy(out=dst, in_=src)
                 else:
@@ -213,29 +220,36 @@ def tile_hopfieldlayer_pa_t_kernel(tc, x, patterns, out):
         x_copy(0, False)
         ptp = transposes(lambda r: p_sb[:, 2 + r // T, r % T, :])
         nc.vector.tensor_copy(out=pt[:, 2:4, :].rearrange("n f (t p) -> n (f t) p", p=P), in_=ptp[:])
-        st_g(-NG)
-        st_g(-NG + 1)
+        issued = [-NG]
+
+        def issue(n):
+            for r in range(n):
+                if issued[0] < NT:
+                    st_g(issued[0])
+                    issued[0] += 1
+
+        issue(6)
 
         def live(q):
             return 0 <= q < NQ
 
         for u in range(LAG - NG // 2, NQ + LAG):
             w = u - LAG
-            vector_helps = u < 1 or u >= NQ + 3 or (u >= LAG and u % HELP == 3)
+            help_step = LAG <= u < NQ and u % HELP == 3
+            if help_step:
+                st_h(2 * w, True)
+                issue(1)
             if live(u):
                 st_b(2 * u)
             if live(u - 2):
                 st_e1(u - 2)
-            if u % 2 == 0 and live(u - 3):
-                st_f((u - 4) // 2)
-            if live(u - 2):
-                st_e2(u - 2)
+            if u >= NQ:
+                if u % 2 == 0 and live(u - 3):
+                    st_f((u - 4) // 2)
+                if live(u - 2):
+                    st_e2(u - 2)
             if u % 2 == 0 and 0 <= u // 2 < F:
                 gram_quant(u // 2)
-            if live(u):
-                st_b(2 * u + 1)
-            if u % 4 == 1 and 0 < (u + 3) // 4 < NB // 2:
-                x_copy((u + 3) // 4, True)
             if live(u - 1):
                 st_c(2 * u - 2)
             if -1 <= u < NQ - 1:
@@ -243,19 +257,31 @@ def tile_hopfieldlayer_pa_t_kernel(tc, x, patterns, out):
             if u == NQ:
                 st_c(2 * u - 1)
                 st_d(u - 1)
-            st_h(2 * w, False)
-            st_g(2 * w + 2)
+            if not help_step:
+                st_h(2 * w, False)
+                if 2 * w >= 4 - NG:
+                    issue(3 if u == NQ else 1)
+            if live(u):
+                st_b(2 * u + 1)
+            if u < NQ:
+                if u % 2 == 0 and live(u - 3):
+                    st_f((u - 4) // 2)
+                if live(u - 2):
+                    st_e2(u - 2)
+            if u % 4 == 1 and 0 < (u + 3) // 4 < NB // 2:
+                x_copy((u + 3) // 4, True)
             if live(u - 1) and u < NQ:
                 st_c(2 * u - 1)
                 st_d(u - 1)
             if -1 <= u < NQ - 1:
                 st_a(2 * u + 3)
-            st_h(2 * w + 1, vector_helps)
+            st_h(2 * w + 1, u < 1 or u >= NQ + 3)
             if w == NQ - 1:
                 store(w, 0, 1)
                 store(w, 1, 2)
             elif w >= 0:
                 store(w, 0, 2)
-            st_g(2 * w + 3)
+            if 2 * w >= 4 - NG:
+                issue(1)
             if u % 4 == 0 and 0 < (u + 4) // 4 < NB // 2:
                 x_transposes((u + 4) // 4)

@@ -22,6 +22,7 @@ NG = F * T
 LAG = 6
 HELP = 5
 WARM = 5
+LENT = 4
 FLOPS = 2 * (B * F * C * N + F * C * C * N + B * F * C * C)
 
 
@@ -32,10 +33,10 @@ def tile_hopfieldlayer_pa_t_kernel(tc, x, patterns, out):
         keep = ctx.enter_context(tc.tile_pool(name="keep", bufs=1))
         work = ctx.enter_context(tc.tile_pool(name="work", bufs=3))
         small = ctx.enter_context(tc.tile_pool(name="small", bufs=6))
-        outs = ctx.enter_context(tc.tile_pool(name="outs", bufs=4))
-        ps_s = ctx.enter_context(tc.psum_pool(name="ps_s", bufs=4))
-        ps_t = ctx.enter_context(tc.psum_pool(name="ps_t", bufs=2))
-        ps_y = ctx.enter_context(tc.psum_pool(name="ps_y", bufs=2))
+        results = ctx.enter_context(tc.tile_pool(name="results", bufs=4))
+        logit_banks = ctx.enter_context(tc.psum_pool(name="logit_banks", bufs=LENT))
+        flip_banks = ctx.enter_context(tc.psum_pool(name="flip_banks", bufs=2))
+        product_banks = ctx.enter_context(tc.psum_pool(name="product_banks", bufs=2))
 
         x_v = x.rearrange("(p i) f n -> p i (f n)", i=NB)
         p_v = patterns.rearrange("f (t p) n -> p f t n", p=P)
@@ -52,112 +53,122 @@ def tile_hopfieldlayer_pa_t_kernel(tc, x, patterns, out):
 
         ident = keep.tile([P, P], BF16)
         make_identity(nc, ident[:])
-        warm_in = keep.tile([P, 1], F32)
-        warm_out = keep.tile([P, 1], F32)
-        nc.vector.memset(warm_in[:], 0.0)
-        nc.scalar.activation(out=warm_out[:], in_=warm_in[:], func=ACT.Exp)
-
+        one_column = keep.tile([P, 1], F32)
+        unused = keep.tile([P, 1], F32)
+        nc.vector.memset(one_column[:], 0.0)
+        nc.scalar.activation(out=unused[:], in_=one_column[:], func=ACT.Exp)
         zeros = keep.tile([P, C], BF16)
         nc.vector.memset(zeros[:], 0.0)
-        idle = ps_s.tile([P, C], F32, tag="s", name="s")
+        idle = logit_banks.tile([P, C], F32, tag="bank", name="idle")
         for r in range(WARM):
             nc.tensor.matmul(out=idle[:], lhsT=zeros[:, 0:P], rhs=zeros[:], start=True, stop=True)
 
         pt = keep.tile([P, F, C], BF16)
         xt = keep.tile([P, NB, F, P], BF16)
-        g_codes = keep.tile([P, F, C], U32, align_bytes=64)
-        g_scales = keep.tile([P, F, C], U8, align_bytes=64)
+        gram_words = keep.tile([P, F, C], U32, align_bytes=64)
+        gram_scales = keep.tile([P, F, C], U8, align_bytes=64)
 
-        def transposes(src):
-            tp = ps_t.tile([P, 8, P], BF16, tag="tp", name="tp")
-            for r in range(8):
-                nc.tensor.transpose(out=tp[:, r, :], in_=src(r), identity=ident[:])
-            return tp
+        def flip(blocks):
+            bank = flip_banks.tile([P, 2 * T, P], BF16, tag="bank", name="flipped")
+            for r in range(2 * T):
+                nc.tensor.transpose(out=bank[:, r, :], in_=blocks(r), identity=ident[:])
+            return bank
 
-        xtp = {}
+        xt_ps, s_ps, neg_max, sums, e_sb, et_ps, et_sb, grouped = {}, {}, {}, {}, {}, {}, {}, {}
+        words, scales, inv_sums, y_ps, o_sb, gram_grouped = {}, {}, {}, {}, {}, {}
 
-        def x_transposes(ii):
-            xtp[ii] = transposes(lambda r: x_sb[:, 2 * ii + r // F, (r % F) * N : (r % F + 1) * N])
+        def flip_x(h):
+            xt_ps[h] = flip(lambda r: x_sb[:, 2 * h + r // F, (r % F) * N : (r % F + 1) * N])
 
-        def x_copy(ii, on_vector):
-            dst = xt[:, 2 * ii : 2 * ii + 2].rearrange("n i f b -> n (i f) b")
+        def unload_x(h, on_vector):
+            dst = xt[:, 2 * h : 2 * h + 2].rearrange("n i f p -> n (i f) p")
             if on_vector:
-                nc.vector.tensor_copy(out=dst, in_=xtp[ii][:])
+                nc.vector.tensor_copy(out=dst, in_=xt_ps[h][:])
             else:
-                nc.scalar.copy(out=dst, in_=xtp[ii][:])
+                nc.scalar.copy(out=dst, in_=xt_ps[h][:])
 
-        s_ps, mn, ssum, e_sb, et_ps, grp, codes, scales, rs, y_ps, o_sb, gg, stg = {}, {}, {}, {}, {}, {}, {}, {}, {}, {}, {}, {}, {}
+        def flip_patterns(h):
+            bank = flip(lambda r: p_sb[:, 2 * h + r // T, r % T, :])
+            nc.vector.tensor_copy(out=pt[:, 2 * h : 2 * h + 2, :].rearrange("n f (t p) -> n (f t) p", p=P), in_=bank[:])
 
-        def st_a(k):
-            i, f = k // F, k % F
-            s_ps[k] = ps_s.tile([P, C], F32, tag="s", name="s")
-            nc.tensor.matmul(out=s_ps[k][:], lhsT=xt[:, i, f, :], rhs=pt[:, f, :], start=True, stop=True)
+        def logits(k):
+            s_ps[k] = logit_banks.tile([P, C], F32, tag="bank", name="s")
+            nc.tensor.matmul(out=s_ps[k][:], lhsT=xt[:, k // F, k % F, :], rhs=pt[:, k % F, :], start=True, stop=True)
 
-        def st_b(k):
+        def negated_max(k):
             q, j = k // 2, k % 2
             if j == 0:
-                mn[q] = small.tile([P, 2], F32, tag="mn", name="mn")
-            nc.vector.tensor_reduce(out=mn[q][:, j : j + 1], in_=s_ps[k][:], axis=AX.X, op=ALU.max, negate=True)
+                neg_max[q] = small.tile([P, 2], F32, tag="neg_max", name="neg_max")
+            nc.vector.tensor_reduce(out=neg_max[q][:, j : j + 1], in_=s_ps[k][:], axis=AX.X, op=ALU.max, negate=True)
 
-        def st_c(k):
+        def exponentials(k):
             q, j = k // 2, k % 2
             if j == 0:
                 e_sb[q] = work.tile([P, 2 * T, P], BF16, tag="e", name="e")
             if k % F == 0:
-                ssum[k // F] = small.tile([P, F], F32, tag="ssum", name="ssum")
+                sums[k // F] = small.tile([P, F], F32, tag="sums", name="sums")
             nc.scalar.activation(
                 out=e_sb[q][:, j * T : (j + 1) * T, :].rearrange("b t p -> b (t p)"),
                 in_=s_ps[k][:],
                 func=ACT.Exp,
-                bias=mn[q][:, j : j + 1],
+                bias=neg_max[q][:, j : j + 1],
                 scale=1.0,
-                accum_out=ssum[k // F][:, k % F : k % F + 1],
+                accum_out=sums[k // F][:, k % F : k % F + 1],
             )
 
-        def st_d(q):
-            et_ps[q] = transposes(lambda r: e_sb[q][:, r, :])
+        def flip_pair(q):
+            et_ps[q] = flip(lambda r: e_sb[q][:, r, :])
 
-        def st_e1(q):
-            if q == NQ - 1:
-                return
-            stg[q] = work.tile([P, 2 * T, P], BF16, tag="stg", name="stg", bufs=2)
-            nc.vector.tensor_copy(out=stg[q][:], in_=et_ps[q][:])
+        def unload_pair(q):
+            if q < NQ - 1:
+                et_sb[q] = work.tile([P, 2 * T, P], BF16, tag="et", name="et", bufs=2)
+                nc.vector.tensor_copy(out=et_sb[q][:], in_=et_ps[q][:])
 
-        def st_e2(q):
+        def regroup_pair(q):
             i, h = q // 2, q % 2
             if h == 0:
-                grp[i] = work.tile([P, F, P, T], BF16, tag="grp", name="grp", align_bytes=64, bufs=1)
-            if q == NQ - 1:
-                nc.vector.tensor_copy(
-                    out=grp[i][:, 2 * h : 2 * h + 2], in_=et_ps[q][:].rearrange("p (j t) b -> p j b t", t=T)
+                grouped[i] = work.tile([P, F, P, T], BF16, tag="grouped", name="grouped", align_bytes=64, bufs=1)
+            dst = grouped[i][:, 2 * h : 2 * h + 2]
+            if q < NQ - 1:
+                nc.gpsimd.tensor_scalar(
+                    out=dst,
+                    in0=et_sb[q][:].rearrange("p (j t) b -> p j b t", t=T),
+                    scalar1=1.0,
+                    scalar2=0.0,
+                    op0=ALU.mult,
+                    op1=ALU.add,
                 )
-                return
-            nc.gpsimd.tensor_scalar(
-                out=grp[i][:, 2 * h : 2 * h + 2],
-                in0=stg[q][:].rearrange("p (j t) b -> p j b t", t=T),
-                scalar1=1.0,
-                scalar2=0.0,
-                op0=ALU.mult,
-                op1=ALU.add,
-            )
+            else:
+                nc.vector.tensor_copy(out=dst, in_=et_ps[q][:].rearrange("p (j t) b -> p j b t", t=T))
 
-        def st_f(i):
-            codes[i] = work.tile([P, F * P], U32, tag="codes", name="codes", align_bytes=64)
+        def quantise_group(i):
+            words[i] = work.tile([P, F * P], U32, tag="words", name="words", align_bytes=64)
             scales[i] = work.tile([P, F * P], U8, tag="scales", name="scales", align_bytes=64)
             nc.vector.quantize_mx(
-                out=codes[i][:].bitcast(FP8X4),
+                out=words[i][:].bitcast(FP8X4),
                 scales=scales[i][:],
-                in_=grp[i][:].rearrange("p f b t -> p (f b t)"),
+                in_=grouped[i][:].rearrange("p f b t -> p (f b t)"),
             )
-            rs[i] = small.tile([P, F], F32, tag="rs", name="rs")
-            nc.vector.reciprocal(out=rs[i][:], in_=ssum[i][:])
+            inv_sums[i] = small.tile([P, F], F32, tag="inv_sums", name="inv_sums")
+            nc.vector.reciprocal(out=inv_sums[i][:], in_=sums[i][:])
 
-        def st_g(k):
-            if k < 4 - NG or k >= NT - 2 * LAG + 2:
-                y_ps[k] = ps_s.tile([P, C], F32, tag="s", name="s")
+        def product(k):
+            if k < LENT - NG or k >= NT - 2 * LAG + 2:
+                y_ps[k] = logit_banks.tile([P, C], F32, tag="bank", name="y")
             else:
-                y_ps[k] = ps_y.tile([P, C], F32, tag="y", name="y")
-            if k < 0:
+                y_ps[k] = product_banks.tile([P, C], F32, tag="bank", name="y")
+            if k >= 0:
+                i, f = k // F, k % F
+                nc.tensor.matmul_mx(
+                    out=y_ps[k][:],
+                    lhsT=words[i][:, f * P : (f + 1) * P].bitcast(FP8X4),
+                    lhsT_scale=scales[i][:, f * P : (f + 1) * P],
+                    rhs=gram_words[:, f, :].bitcast(FP8X4),
+                    rhs_scale=gram_scales[:, f, :],
+                    start=True,
+                    stop=True,
+                )
+            else:
                 f, cb = (k + NG) // T, (k + NG) % T
                 for t in range(T):
                     nc.tensor.matmul(
@@ -167,121 +178,108 @@ def tile_hopfieldlayer_pa_t_kernel(tc, x, patterns, out):
                         start=True,
                         stop=True,
                     )
-                return
-            f = k % F
-            nc.tensor.matmul_mx(
-                out=y_ps[k][:],
-                lhsT=codes[k // F][:, f * P : (f + 1) * P].bitcast(FP8X4),
-                lhsT_scale=scales[k // F][:, f * P : (f + 1) * P],
-                rhs=g_codes[:, f, :].bitcast(FP8X4),
-                rhs_scale=g_scales[:, f, :],
-                start=True,
-                stop=True,
-            )
 
-        def st_h(k, on_vector):
-            if k < -NG:
-                return
-            if k < 0:
+        issued = [-NG]
+
+        def products(n):
+            for r in range(n):
+                if issued[0] < NT:
+                    product(issued[0])
+                    issued[0] += 1
+
+        def leave(k, on_vector):
+            if k >= 0:
+                q, j = k // 2, k % 2
+                if j == 0:
+                    o_sb[q] = results.tile([P, 2, C], F32, tag="o", name="o")
+                dst, src, factor = o_sb[q][:, j, :], y_ps[k][:], inv_sums[k // F][:, k % F : k % F + 1]
+                if on_vector:
+                    nc.vector.tensor_scalar_mul(out=dst, in0=src, scalar1=factor)
+                else:
+                    nc.scalar.activation(out=dst, in_=src, func=ACT.Copy, scale=factor)
+            else:
                 f, cb = (k + NG) // T, (k + NG) % T
                 if cb == 0:
-                    gg[f] = work.tile([P, C, T], BF16, tag="gg", name="gg", align_bytes=64, bufs=2)
-                dst = gg[f][:, cb * P : (cb + 1) * P, :]
+                    gram_grouped[f] = work.tile([P, C, T], BF16, tag="gram", name="gram", align_bytes=64, bufs=2)
+                dst = gram_grouped[f][:, cb * P : (cb + 1) * P, :]
                 src = y_ps[k][:].rearrange("p (t c) -> p c t", t=T)
                 if on_vector:
                     nc.vector.tensor_copy(out=dst, in_=src)
                 else:
                     nc.scalar.copy(out=dst, in_=src)
-                return
-            q, j = k // 2, k % 2
-            if j == 0:
-                o_sb[q] = outs.tile([P, 2, C], F32, tag="o", name="o")
-            if on_vector:
-                nc.vector.tensor_scalar_mul(out=o_sb[q][:, j, :], in0=y_ps[k][:], scalar1=rs[k // F][:, k % F : k % F + 1])
-            else:
-                nc.scalar.activation(
-                    out=o_sb[q][:, j, :], in_=y_ps[k][:], func=ACT.Copy, scale=rs[k // F][:, k % F : k % F + 1]
-                )
 
-        def gram_quant(f):
+        def quantise_gram(f):
             nc.vector.quantize_mx(
-                out=g_codes[:, f, :].bitcast(FP8X4),
-                scales=g_scales[:, f, :],
-                in_=gg[f][:].rearrange("p c t -> p (c t)"),
+                out=gram_words[:, f, :].bitcast(FP8X4),
+                scales=gram_scales[:, f, :],
+                in_=gram_grouped[f][:].rearrange("p c t -> p (c t)"),
             )
 
         def store(q, j0, j1):
-            i, f0 = q // 2, 2 * (q % 2)
-            nc.sync.dma_start(out=out_v[:, i, f0 + j0 : f0 + j1, :], in_=o_sb[q][:, j0:j1, :])
+            nc.sync.dma_start(out=out_v[:, q // 2, 2 * (q % 2) + j0 : 2 * (q % 2) + j1, :], in_=o_sb[q][:, j0:j1, :])
 
-        ptp = transposes(lambda r: p_sb[:, r // T, r % T, :])
-        nc.vector.tensor_copy(out=pt[:, 0:2, :].rearrange("n f (t p) -> n (f t) p", p=P), in_=ptp[:])
-        x_transposes(0)
-        x_copy(0, False)
-        ptp = transposes(lambda r: p_sb[:, 2 + r // T, r % T, :])
-        nc.vector.tensor_copy(out=pt[:, 2:4, :].rearrange("n f (t p) -> n (f t) p", p=P), in_=ptp[:])
-        issued = [-NG]
-
-        def issue(n):
-            for r in range(n):
-                if issued[0] < NT:
-                    st_g(issued[0])
-                    issued[0] += 1
-
-        issue(6)
-
-        def live(q):
+        def pair(q):
             return 0 <= q < NQ
 
+        flip_patterns(0)
+        flip_x(0)
+        unload_x(0, False)
+        flip_patterns(1)
+        products(LENT + 2)
+
         for u in range(LAG - NG // 2, NQ + LAG):
-            w = u - LAG
+            first, second = 2 * (u - LAG), 2 * (u - LAG) + 1
+            bank_returns = first >= LENT - NG
             help_step = LAG <= u < NQ and u % HELP == 3
+            draining = u >= NQ
+            group_done = u % 2 == 0 and pair(u - 3)
+
             if help_step:
-                st_h(2 * w, True)
-                issue(1)
-            if live(u):
-                st_b(2 * u)
-            if live(u - 2):
-                st_e1(u - 2)
-            if u >= NQ:
-                if u % 2 == 0 and live(u - 3):
-                    st_f((u - 4) // 2)
-                if live(u - 2):
-                    st_e2(u - 2)
+                leave(first, True)
+                products(1)
+            if pair(u):
+                negated_max(2 * u)
+            if pair(u - 2):
+                unload_pair(u - 2)
+            if draining and group_done:
+                quantise_group((u - 4) // 2)
+            if draining and pair(u - 2):
+                regroup_pair(u - 2)
             if u % 2 == 0 and 0 <= u // 2 < F:
-                gram_quant(u // 2)
-            if live(u - 1):
-                st_c(2 * u - 2)
+                quantise_gram(u // 2)
+            if pair(u - 1):
+                exponentials(2 * u - 2)
             if -1 <= u < NQ - 1:
-                st_a(2 * u + 2)
+                logits(2 * u + 2)
             if u == NQ:
-                st_c(2 * u - 1)
-                st_d(u - 1)
+                products(2)
+                exponentials(2 * u - 1)
+                flip_pair(u - 1)
             if not help_step:
-                st_h(2 * w, False)
-                if 2 * w >= 4 - NG:
-                    issue(3 if u == NQ else 1)
-            if live(u):
-                st_b(2 * u + 1)
-            if u < NQ:
-                if u % 2 == 0 and live(u - 3):
-                    st_f((u - 4) // 2)
-                if live(u - 2):
-                    st_e2(u - 2)
+                leave(first, False)
+                if bank_returns:
+                    products(1)
+
+            if pair(u):
+                negated_max(2 * u + 1)
+            if not draining and group_done:
+                quantise_group((u - 4) // 2)
+            if not draining and pair(u - 2):
+                regroup_pair(u - 2)
             if u % 4 == 1 and 0 < (u + 3) // 4 < NB // 2:
-                x_copy((u + 3) // 4, True)
-            if live(u - 1) and u < NQ:
-                st_c(2 * u - 1)
-                st_d(u - 1)
+                unload_x((u + 3) // 4, True)
+            if pair(u - 1) and u < NQ:
+                exponentials(2 * u - 1)
+                flip_pair(u - 1)
             if -1 <= u < NQ - 1:
-                st_a(2 * u + 3)
-            st_h(2 * w + 1, u < 1 or u >= NQ + 3)
-            if w == NQ - 1:
-                store(w, 0, 1)
-                store(w, 1, 2)
-            elif w >= 0:
-                store(w, 0, 2)
-            if 2 * w >= 4 - NG:
-                issue(1)
+                logits(2 * u + 3)
+            leave(second, u < 1 or u >= NQ + 3)
+            if second == NT - 1:
+                store(second // 2, 0, 1)
+                store(second // 2, 1, 2)
+            elif second > 0:
+                store(second // 2, 0, 2)
+            if bank_returns:
+                products(1)
             if u % 4 == 0 and 0 < (u + 4) // 4 < NB // 2:
-                x_transposes((u + 4) // 4)
+                flip_x((u + 4) // 4)

@@ -20,7 +20,7 @@ NT = NB * F
 NQ = NT // 2
 NG = F * T
 LAG = 6
-HELP = 5
+HELP = 8
 WARM = 5
 LENT = 4
 FLOPS = 2 * (B * F * C * N + F * C * C * N + B * F * C * C)
@@ -91,29 +91,29 @@ def tile_hopfieldlayer_pa_t_kernel(tc, x, patterns, out):
             bank = flip(lambda r: p_sb[:, 2 * h + r // T, r % T, :])
             nc.vector.tensor_copy(out=pt[:, 2 * h : 2 * h + 2, :].rearrange("n f (t p) -> n (f t) p", p=P), in_=bank[:])
 
-        def logits(k):
-            s_ps[k] = logit_banks.tile([P, C], F32, tag="bank", name="s")
-            nc.tensor.matmul(out=s_ps[k][:], lhsT=xt[:, k // F, k % F, :], rhs=pt[:, k % F, :], start=True, stop=True)
+        def logits(m):
+            s_ps[m] = logit_banks.tile([P, C], F32, tag="bank", name="s")
+            nc.tensor.matmul(out=s_ps[m][:], lhsT=xt[:, m // F, m % F, :], rhs=pt[:, m % F, :], start=True, stop=True)
 
-        def negated_max(k):
-            q, j = k // 2, k % 2
+        def negated_max(m):
+            q, j = m // 2, m % 2
             if j == 0:
                 neg_max[q] = small.tile([P, 2], F32, tag="neg_max", name="neg_max")
-            nc.vector.tensor_reduce(out=neg_max[q][:, j : j + 1], in_=s_ps[k][:], axis=AX.X, op=ALU.max, negate=True)
+            nc.vector.tensor_reduce(out=neg_max[q][:, j : j + 1], in_=s_ps[m][:], axis=AX.X, op=ALU.max, negate=True)
 
-        def exponentials(k):
-            q, j = k // 2, k % 2
+        def exponentials(m):
+            q, j = m // 2, m % 2
             if j == 0:
                 e_sb[q] = work.tile([P, 2 * T, P], BF16, tag="e", name="e")
-            if k % F == 0:
-                sums[k // F] = small.tile([P, F], F32, tag="sums", name="sums")
+            if m % F == 0:
+                sums[m // F] = small.tile([P, F], F32, tag="sums", name="sums")
             nc.scalar.activation(
                 out=e_sb[q][:, j * T : (j + 1) * T, :].rearrange("b t p -> b (t p)"),
-                in_=s_ps[k][:],
+                in_=s_ps[m][:],
                 func=ACT.Exp,
                 bias=neg_max[q][:, j : j + 1],
                 scale=1.0,
-                accum_out=sums[k // F][:, k % F : k % F + 1],
+                accum_out=sums[m // F][:, m % F : m % F + 1],
             )
 
         def flip_pair(q):
@@ -125,10 +125,10 @@ def tile_hopfieldlayer_pa_t_kernel(tc, x, patterns, out):
                 nc.vector.tensor_copy(out=et_sb[q][:], in_=et_ps[q][:])
 
         def regroup_pair(q):
-            i, h = q // 2, q % 2
-            if h == 0:
+            i, f0 = q // 2, 2 * (q % 2)
+            if f0 == 0:
                 grouped[i] = work.tile([P, F, P, T], BF16, tag="grouped", name="grouped", align_bytes=64, bufs=1)
-            dst = grouped[i][:, 2 * h : 2 * h + 2]
+            dst = grouped[i][:, f0 : f0 + 2]
             if q < NQ - 1:
                 nc.gpsimd.tensor_scalar(
                     out=dst,
@@ -152,15 +152,15 @@ def tile_hopfieldlayer_pa_t_kernel(tc, x, patterns, out):
             inv_sums[i] = small.tile([P, F], F32, tag="inv_sums", name="inv_sums")
             nc.vector.reciprocal(out=inv_sums[i][:], in_=sums[i][:])
 
-        def product(k):
-            if k < LENT - NG or k >= NT - 2 * LAG + 2:
-                y_ps[k] = logit_banks.tile([P, C], F32, tag="bank", name="y")
+        def product(m):
+            if m < LENT - NG or m >= NT - 2 * LAG + 2:
+                y_ps[m] = logit_banks.tile([P, C], F32, tag="bank", name="y")
             else:
-                y_ps[k] = product_banks.tile([P, C], F32, tag="bank", name="y")
-            if k >= 0:
-                i, f = k // F, k % F
+                y_ps[m] = product_banks.tile([P, C], F32, tag="bank", name="y")
+            if m >= 0:
+                i, f = m // F, m % F
                 nc.tensor.matmul_mx(
-                    out=y_ps[k][:],
+                    out=y_ps[m][:],
                     lhsT=words[i][:, f * P : (f + 1) * P].bitcast(FP8X4),
                     lhsT_scale=scales[i][:, f * P : (f + 1) * P],
                     rhs=gram_words[:, f, :].bitcast(FP8X4),
@@ -169,10 +169,10 @@ def tile_hopfieldlayer_pa_t_kernel(tc, x, patterns, out):
                     stop=True,
                 )
             else:
-                f, cb = (k + NG) // T, (k + NG) % T
+                f, cb = (m + NG) // T, (m + NG) % T
                 for t in range(T):
                     nc.tensor.matmul(
-                        out=y_ps[k][:, t * P : (t + 1) * P],
+                        out=y_ps[m][:, t * P : (t + 1) * P],
                         lhsT=pt[:, f, t * P : (t + 1) * P],
                         rhs=pt[:, f, cb * P : (cb + 1) * P],
                         start=True,
@@ -187,22 +187,22 @@ def tile_hopfieldlayer_pa_t_kernel(tc, x, patterns, out):
                     product(issued[0])
                     issued[0] += 1
 
-        def leave(k, on_vector):
-            if k >= 0:
-                q, j = k // 2, k % 2
+        def leave(m, on_vector):
+            if m >= 0:
+                q, j = m // 2, m % 2
                 if j == 0:
                     o_sb[q] = results.tile([P, 2, C], F32, tag="o", name="o")
-                dst, src, factor = o_sb[q][:, j, :], y_ps[k][:], inv_sums[k // F][:, k % F : k % F + 1]
+                dst, src, factor = o_sb[q][:, j, :], y_ps[m][:], inv_sums[m // F][:, m % F : m % F + 1]
                 if on_vector:
                     nc.vector.tensor_scalar_mul(out=dst, in0=src, scalar1=factor)
                 else:
                     nc.scalar.activation(out=dst, in_=src, func=ACT.Copy, scale=factor)
             else:
-                f, cb = (k + NG) // T, (k + NG) % T
+                f, cb = (m + NG) // T, (m + NG) % T
                 if cb == 0:
                     gram_grouped[f] = work.tile([P, C, T], BF16, tag="gram", name="gram", align_bytes=64, bufs=2)
                 dst = gram_grouped[f][:, cb * P : (cb + 1) * P, :]
-                src = y_ps[k][:].rearrange("p (t c) -> p c t", t=T)
+                src = y_ps[m][:].rearrange("p (t c) -> p c t", t=T)
                 if on_vector:
                     nc.vector.tensor_copy(out=dst, in_=src)
                 else:
@@ -229,7 +229,7 @@ def tile_hopfieldlayer_pa_t_kernel(tc, x, patterns, out):
 
         for u in range(LAG - NG // 2, NQ + LAG):
             first, second = 2 * (u - LAG), 2 * (u - LAG) + 1
-            bank_returns = first >= LENT - NG
+            refill = first >= LENT - NG
             help_step = LAG <= u < NQ and u % HELP == 3
             draining = u >= NQ
             group_done = u % 2 == 0 and pair(u - 3)
@@ -257,7 +257,7 @@ def tile_hopfieldlayer_pa_t_kernel(tc, x, patterns, out):
                 flip_pair(u - 1)
             if not help_step:
                 leave(first, False)
-                if bank_returns:
+                if refill:
                     products(1)
 
             if pair(u):
@@ -279,7 +279,7 @@ def tile_hopfieldlayer_pa_t_kernel(tc, x, patterns, out):
                 store(second // 2, 1, 2)
             elif second > 0:
                 store(second // 2, 0, 2)
-            if bank_returns:
+            if refill:
                 products(1)
             if u % 4 == 0 and 0 < (u + 4) // 4 < NB // 2:
                 flip_x((u + 4) // 4)

@@ -20,7 +20,6 @@ NT = NB * F
 NQ = NT // 2
 NG = F * T
 LAG = 6
-HELP = 8
 WARM = 5
 LENT = 4
 FLOPS = 2 * (B * F * C * N + F * C * C * N + B * F * C * C)
@@ -230,13 +229,9 @@ def tile_hopfieldlayer_pa_t_kernel(tc, x, patterns, out):
         for u in range(LAG - NG // 2, NQ + LAG):
             first, second = 2 * (u - LAG), 2 * (u - LAG) + 1
             refill = first >= LENT - NG
-            help_step = LAG <= u < NQ and u % HELP == 3
             draining = u >= NQ
             group_done = u % 2 == 0 and pair(u - 3)
 
-            if help_step:
-                leave(first, True)
-                products(1)
             if pair(u):
                 negated_max(2 * u)
             if pair(u - 2):
@@ -255,10 +250,9 @@ def tile_hopfieldlayer_pa_t_kernel(tc, x, patterns, out):
                 products(2)
                 exponentials(2 * u - 1)
                 flip_pair(u - 1)
-            if not help_step:
-                leave(first, False)
-                if refill:
-                    products(1)
+            leave(first, False)
+            if refill:
+                products(1)
 
             if pair(u):
                 negated_max(2 * u + 1)

from contextlib import ExitStack

import concourse.mybir as mybir
from concourse.masks import make_identity

F32 = mybir.dt.float32
BF16 = mybir.dt.bfloat16
U32 = mybir.dt.uint32
U8 = mybir.dt.uint8
FP8X4 = mybir.dt.float8_e4m3fn_x4
ACT = mybir.ActivationFunctionType
ALU = mybir.AluOpType
AX = mybir.AxisListType

P = 128
B, F, C, N = 2048, 4, 512, 128
T = C // P
NB = B // P
NT = NB * F
NQ = NT // 2
NG = F * T
LAG = 6
WARM = 5
LENT = 4
FLOPS = 2 * (B * F * C * N + F * C * C * N + B * F * C * C)


def tile_hopfieldlayer_pa_t_kernel(tc, x, patterns, out):
    nc = tc.nc
    with ExitStack() as ctx:
        ctx.enter_context(tc.manual_schedule())
        keep = ctx.enter_context(tc.tile_pool(name="keep", bufs=1))
        work = ctx.enter_context(tc.tile_pool(name="work", bufs=3))
        small = ctx.enter_context(tc.tile_pool(name="small", bufs=6))
        results = ctx.enter_context(tc.tile_pool(name="results", bufs=4))
        logit_banks = ctx.enter_context(tc.psum_pool(name="logit_banks", bufs=LENT))
        flip_banks = ctx.enter_context(tc.psum_pool(name="flip_banks", bufs=2))
        product_banks = ctx.enter_context(tc.psum_pool(name="product_banks", bufs=2))

        x_v = x.rearrange("(p i) f n -> p i (f n)", i=NB)
        p_v = patterns.rearrange("f (t p) n -> p f t n", p=P)
        out_v = out.rearrange("(p i) f c -> p i f c", i=NB)

        p_sb = keep.tile([P, F, T, N], BF16)
        x_sb = keep.tile([P, NB, F * N], BF16)
        nc.sync.dma_start(out=p_sb[:, 0:2], in_=p_v[:, 0:2])
        nc.sync.dma_start(out=x_sb[:, 0:2, :], in_=x_v[:, 0:2, :])
        nc.sync.dma_start(out=p_sb[:, 2:4], in_=p_v[:, 2:4])
        nc.sync.dma_start(out=x_sb[:, 2:4, :], in_=x_v[:, 2:4, :])
        for i0 in (4, 8, 12):
            nc.sync.dma_start(out=x_sb[:, i0 : i0 + 4, :], in_=x_v[:, i0 : i0 + 4, :])

        ident = keep.tile([P, P], BF16)
        make_identity(nc, ident[:])
        one_column = keep.tile([P, 1], F32)
        unused = keep.tile([P, 1], F32)
        nc.vector.memset(one_column[:], 0.0)
        nc.scalar.activation(out=unused[:], in_=one_column[:], func=ACT.Exp)
        zeros = keep.tile([P, C], BF16)
        nc.vector.memset(zeros[:], 0.0)
        idle = logit_banks.tile([P, C], F32, tag="bank", name="idle")
        for r in range(WARM):
            nc.tensor.matmul(out=idle[:], lhsT=zeros[:, 0:P], rhs=zeros[:], start=True, stop=True)

        pt = keep.tile([P, F, C], BF16)
        xt = keep.tile([P, NB, F, P], BF16)
        gram_words = keep.tile([P, F, C], U32, align_bytes=64)
        gram_scales = keep.tile([P, F, C], U8, align_bytes=64)

        def flip(blocks):
            bank = flip_banks.tile([P, 2 * T, P], BF16, tag="bank", name="flipped")
            for r in range(2 * T):
                nc.tensor.transpose(out=bank[:, r, :], in_=blocks(r), identity=ident[:])
            return bank

        xt_ps, s_ps, neg_max, sums, e_sb, et_ps, et_sb, grouped = {}, {}, {}, {}, {}, {}, {}, {}
        words, scales, inv_sums, y_ps, o_sb, gram_grouped = {}, {}, {}, {}, {}, {}

        def flip_x(h):
            xt_ps[h] = flip(lambda r: x_sb[:, 2 * h + r // F, (r % F) * N : (r % F + 1) * N])

        def unload_x(h, on_vector):
            dst = xt[:, 2 * h : 2 * h + 2].rearrange("n i f p -> n (i f) p")
            if on_vector:
                nc.vector.tensor_copy(out=dst, in_=xt_ps[h][:])
            else:
                nc.scalar.copy(out=dst, in_=xt_ps[h][:])

        def flip_patterns(h):
            bank = flip(lambda r: p_sb[:, 2 * h + r // T, r % T, :])
            nc.vector.tensor_copy(out=pt[:, 2 * h : 2 * h + 2, :].rearrange("n f (t p) -> n (f t) p", p=P), in_=bank[:])

        def logits(m):
            s_ps[m] = logit_banks.tile([P, C], F32, tag="bank", name="s")
            nc.tensor.matmul(out=s_ps[m][:], lhsT=xt[:, m // F, m % F, :], rhs=pt[:, m % F, :], start=True, stop=True)

        def negated_max(m):
            q, j = m // 2, m % 2
            if j == 0:
                neg_max[q] = small.tile([P, 2], F32, tag="neg_max", name="neg_max")
            nc.vector.tensor_reduce(out=neg_max[q][:, j : j + 1], in_=s_ps[m][:], axis=AX.X, op=ALU.max, negate=True)

        def exponentials(m):
            q, j = m // 2, m % 2
            if j == 0:
                e_sb[q] = work.tile([P, 2 * T, P], BF16, tag="e", name="e")
            if m % F == 0:
                sums[m // F] = small.tile([P, F], F32, tag="sums", name="sums")
            nc.scalar.activation(
                out=e_sb[q][:, j * T : (j + 1) * T, :].rearrange("b t p -> b (t p)"),
                in_=s_ps[m][:],
                func=ACT.Exp,
                bias=neg_max[q][:, j : j + 1],
                scale=1.0,
                accum_out=sums[m // F][:, m % F : m % F + 1],
            )

        def flip_pair(q):
            et_ps[q] = flip(lambda r: e_sb[q][:, r, :])

        def unload_pair(q):
            if q < NQ - 1:
                et_sb[q] = work.tile([P, 2 * T, P], BF16, tag="et", name="et", bufs=2)
                nc.vector.tensor_copy(out=et_sb[q][:], in_=et_ps[q][:])

        def regroup_pair(q):
            i, f0 = q // 2, 2 * (q % 2)
            if f0 == 0:
                grouped[i] = work.tile([P, F, P, T], BF16, tag="grouped", name="grouped", align_bytes=64, bufs=1)
            dst = grouped[i][:, f0 : f0 + 2]
            if q < NQ - 1:
                nc.gpsimd.tensor_scalar(
                    out=dst,
                    in0=et_sb[q][:].rearrange("p (j t) b -> p j b t", t=T),
                    scalar1=1.0,
                    scalar2=0.0,
                    op0=ALU.mult,
                    op1=ALU.add,
                )
            else:
                nc.vector.tensor_copy(out=dst, in_=et_ps[q][:].rearrange("p (j t) b -> p j b t", t=T))

        def quantise_group(i):
            words[i] = work.tile([P, F * P], U32, tag="words", name="words", align_bytes=64)
            scales[i] = work.tile([P, F * P], U8, tag="scales", name="scales", align_bytes=64)
            nc.vector.quantize_mx(
                out=words[i][:].bitcast(FP8X4),
                scales=scales[i][:],
                in_=grouped[i][:].rearrange("p f b t -> p (f b t)"),
            )
            inv_sums[i] = small.tile([P, F], F32, tag="inv_sums", name="inv_sums")
            nc.vector.reciprocal(out=inv_sums[i][:], in_=sums[i][:])

        def product(m):
            if m < LENT - NG or m >= NT - 2 * LAG + 2:
                y_ps[m] = logit_banks.tile([P, C], F32, tag="bank", name="y")
            else:
                y_ps[m] = product_banks.tile([P, C], F32, tag="bank", name="y")
            if m >= 0:
                i, f = m // F, m % F
                nc.tensor.matmul_mx(
                    out=y_ps[m][:],
                    lhsT=words[i][:, f * P : (f + 1) * P].bitcast(FP8X4),
                    lhsT_scale=scales[i][:, f * P : (f + 1) * P],
                    rhs=gram_words[:, f, :].bitcast(FP8X4),
                    rhs_scale=gram_scales[:, f, :],
                    start=True,
                    stop=True,
                )
            else:
                f, cb = (m + NG) // T, (m + NG) % T
                for t in range(T):
                    nc.tensor.matmul(
                        out=y_ps[m][:, t * P : (t + 1) * P],
                        lhsT=pt[:, f, t * P : (t + 1) * P],
                        rhs=pt[:, f, cb * P : (cb + 1) * P],
                        start=True,
                        stop=True,
                    )

        issued = [-NG]

        def products(n):
            for r in range(n):
                if issued[0] < NT:
                    product(issued[0])
                    issued[0] += 1

        def leave(m, on_vector):
            if m >= 0:
                q, j = m // 2, m % 2
                if j == 0:
                    o_sb[q] = results.tile([P, 2, C], F32, tag="o", name="o")
                dst, src, factor = o_sb[q][:, j, :], y_ps[m][:], inv_sums[m // F][:, m % F : m % F + 1]
                if on_vector:
                    nc.vector.tensor_scalar_mul(out=dst, in0=src, scalar1=factor)
                else:
                    nc.scalar.activation(out=dst, in_=src, func=ACT.Copy, scale=factor)
            else:
                f, cb = (m + NG) // T, (m + NG) % T
                if cb == 0:
                    gram_grouped[f] = work.tile([P, C, T], BF16, tag="gram", name="gram", align_bytes=64, bufs=2)
                dst = gram_grouped[f][:, cb * P : (cb + 1) * P, :]
                src = y_ps[m][:].rearrange("p (t c) -> p c t", t=T)
                if on_vector:
                    nc.vector.tensor_copy(out=dst, in_=src)
                else:
                    nc.scalar.copy(out=dst, in_=src)

        def quantise_gram(f):
            nc.vector.quantize_mx(
                out=gram_words[:, f, :].bitcast(FP8X4),
                scales=gram_scales[:, f, :],
                in_=gram_grouped[f][:].rearrange("p c t -> p (c t)"),
            )

        def store(q, j0, j1):
            nc.sync.dma_start(out=out_v[:, q // 2, 2 * (q % 2) + j0 : 2 * (q % 2) + j1, :], in_=o_sb[q][:, j0:j1, :])

        def pair(q):
            return 0 <= q < NQ

        flip_patterns(0)
        flip_x(0)
        unload_x(0, False)
        flip_patterns(1)
        products(LENT + 2)

        for u in range(LAG - NG // 2, NQ + LAG):
            first, second = 2 * (u - LAG), 2 * (u - LAG) + 1
            refill = first >= LENT - NG
            draining = u >= NQ
            group_done = u % 2 == 0 and pair(u - 3)

            if pair(u):
                negated_max(2 * u)
            if pair(u - 2):
                unload_pair(u - 2)
            if draining and group_done:
                quantise_group((u - 4) // 2)
            if draining and pair(u - 2):
                regroup_pair(u - 2)
            if u % 2 == 0 and 0 <= u // 2 < F:
                quantise_gram(u // 2)
            if pair(u - 1):
                exponentials(2 * u - 2)
            if -1 <= u < NQ - 1:
                logits(2 * u + 2)
            if u == NQ:
                products(2)
                exponentials(2 * u - 1)
                flip_pair(u - 1)
            leave(first, False)
            if refill:
                products(1)

            if pair(u):
                negated_max(2 * u + 1)
            if not draining and group_done:
                quantise_group((u - 4) // 2)
            if not draining and pair(u - 2):
                regroup_pair(u - 2)
            if u % 4 == 1 and 0 < (u + 3) // 4 < NB // 2:
                unload_x((u + 3) // 4, True)
            if pair(u - 1) and u < NQ:
                exponentials(2 * u - 1)
                flip_pair(u - 1)
            if -1 <= u < NQ - 1:
                logits(2 * u + 3)
            leave(second, u < 1 or u >= NQ + 3)
            if second == NT - 1:
                store(second // 2, 0, 1)
                store(second // 2, 1, 2)
            elif second > 0:
                store(second // 2, 0, 2)
            if refill:
                products(1)
            if u % 4 == 0 and 0 < (u + 4) // 4 < NB // 2:
                flip_x((u + 4) // 4)
